import numpy as np
import ml_dtypes


def mxq(x, axis, fmt="e4m3"):
    dtype, down = {"e4m3": (ml_dtypes.float8_e4m3fn, 7), "e5m2": (ml_dtypes.float8_e5m2, 14)}[fmt]
    v = np.moveaxis(np.asarray(x, np.float32).astype(ml_dtypes.bfloat16).astype(np.float64), axis, -1)
    blocks = v.reshape(v.shape[:-1] + (-1, 32))
    amax = np.abs(blocks).max(-1, keepdims=True)
    byte = np.maximum(np.where(amax > 0, np.frexp(amax)[1] - 1 + 127, 0) - down, 1)
    scale = np.exp2(byte - 127.0)
    codes = (blocks / scale).astype(np.float32).astype(dtype).astype(np.float64)
    return np.moveaxis((codes * scale).reshape(v.shape), -1, axis)


WIDE = False


def mx_kscale(k):
    if not WIDE:
        return np.ones(k)
    levels = np.array([10, -10, 5, -5, 0])
    if k % 512:
        return np.exp2(np.random.permutation(np.resize(levels, k // 32))).repeat(32)
    a = np.empty((k // 512, 16))
    for p in range(k // 512):
        a[p, :8] = np.random.permutation(np.resize(levels, 8))
        for g in range(8):
            far = levels[np.abs(levels - a[p, g]) >= 10]
            a[p, g + 8] = far[np.random.randint(len(far))]
    return np.exp2(a.ravel()).repeat(32)


BF16 = ml_dtypes.bfloat16


def bf(x):
    return np.asarray(x, np.float32).astype(BF16)


def f64(x):
    return np.asarray(x).astype(np.float64)


B, F, M, N, H, O = 1, 128, 128, 128, 512, 128
BN_EPS = 1e-5


def bn(x, g, b, m, v):
    sh = [1] * x.ndim
    sh[1] = -1
    return g.reshape(sh) * (x - m.reshape(sh)) * (1.0 / np.sqrt(v.reshape(sh) + BN_EPS)) + b.reshape(sh)


def setup_inputs():
    s = mx_kscale(H)
    k = mx_kscale(H)
    return {"h2": bf(np.maximum(np.random.standard_normal((B, H, M, N)), 0.0) * s[None, :, None, None]),
            "W3": bf(np.random.standard_normal((H, H)) * 1.4 / np.sqrt(H) / s[None, :]),
            "g3": bf((1.0 + 0.1 * np.random.standard_normal(H)) * k),
            "b3": bf(0.2 * np.random.standard_normal(H) * k),
            "m3": bf(0.2 * np.random.standard_normal(H)),
            "v3": bf(np.random.uniform(0.5, 1.5, H)),
            "Wc1": bf(np.random.standard_normal((H, H)) * 0.4 / np.sqrt(H) / k[None, :]),
            "gc1": bf(1.0 + 0.1 * np.random.standard_normal(H)),
            "bc1": bf(0.2 * np.random.standard_normal(H)),
            "mc1": bf(0.2 * np.random.standard_normal(H)),
            "vc1": bf(np.random.uniform(0.5, 1.5, H))}


def reference(h2, W3, g3, b3, m3, v3, Wc1, gc1, bc1, mc1, vc1):
    x3 = f64(bf(mxq(f64(W3), 1, "e4m3") @ mxq(f64(h2).reshape(B, H, M * N), 1, "e4m3"))).reshape(B, H, M, N)
    h3 = np.maximum(bn(x3, f64(g3), f64(b3), f64(m3), f64(v3)), 0.0)
    p = h3.max(axis=2)
    xc = mxq(f64(Wc1), 1, "e4m3") @ mxq(p, 1, "e4m3")
    return np.maximum(bn(xc, f64(gc1), f64(bc1), f64(mc1), f64(vc1)), 0.0)

@@ -1,0 +1,288 @@
+from contextlib import ExitStack
+
+import concourse.mybir as mybir
+from concourse.masks import make_identity
+
+F32 = mybir.dt.float32
+BF16 = mybir.dt.bfloat16
+U32 = mybir.dt.uint32
+U8 = mybir.dt.uint8
+FP8X4 = mybir.dt.float8_e4m3fn_x4
+ALU = mybir.AluOpType
+ACT = mybir.ActivationFunctionType
+
+P = 128
+PACK = 4
+H = 512
+NPTS = 128
+COLS = NPTS * NPTS
+UNIT = 512
+UNITS = COLS // UNIT
+SHORT_LOADS = 6
+LOADS = (UNIT,) * SHORT_LOADS + (2 * UNIT,) * ((UNITS - SHORT_LOADS) // 2)
+WC1_LOAD_AT = 12 * UNIT
+BANKS = UNITS * PACK
+AHEAD = 6
+GROUPED_BUFS = 2
+S_COLS = 336
+BN_EPS = 1e-5
+WC1_AT = 48
+
+FLOPS = 2 * H * H * (COLS + NPTS)
+
+
+def tile_p2b_xcorr_pb_kernel(tc, h2, W3, g3, b3, m3, v3, Wc1, gc1, bc1, mc1, vc1, out):
+    nc = tc.nc
+    with ExitStack() as ctx:
+        keep = ctx.enter_context(tc.tile_pool(name="keep", bufs=1))
+        rawp = ctx.enter_context(tc.tile_pool(name="rawp", bufs=1))
+        grpp = ctx.enter_context(tc.tile_pool(name="grpp", bufs=GROUPED_BUFS))
+        codp = ctx.enter_context(tc.tile_pool(name="codp", bufs=3))
+        psum = ctx.enter_context(tc.psum_pool(name="psum", bufs=AHEAD))
+        ctx.enter_context(tc.manual_schedule())
+
+        prm = keep.tile([P, 8, 16], BF16)
+
+        def load_vector(queue, slot, vec):
+            queue.dma_start(out=prm[:, slot, 0:PACK], in_=vec.rearrange("(p t) -> p t", t=PACK))
+
+        load_vector(nc.scalar, 0, g3)
+        load_vector(nc.scalar, 6, v3)
+        load_vector(nc.scalar, 2, b3)
+        load_vector(nc.scalar, 4, m3)
+
+        ident = keep.tile([P, P], F32)
+        make_identity(nc, ident[:])
+        load_vector(nc.gpsimd, 7, vc1)
+        load_vector(nc.gpsimd, 1, gc1)
+        load_vector(nc.gpsimd, 3, bc1)
+        load_vector(nc.gpsimd, 5, mc1)
+
+        w3_rows = keep.tile([P, PACK, H], BF16)
+        nc.sync.dma_start(out=w3_rows[:], in_=W3.rearrange("(m t) h -> m t h", t=PACK))
+        wc1_rows = keep.tile([P, PACK, H], BF16)
+
+        h2_rows = h2[0].rearrange("(p j) m n -> p j (m n)", j=PACK)
+        raw_of = {}
+        first = 0
+        for width in LOADS:
+            raw = rawp.tile([P, PACK, width], BF16, tag="raw%d" % width, bufs=SHORT_LOADS if width == UNIT else len(LOADS) - SHORT_LOADS)
+            nc.sync.dma_start(out=raw[:], in_=h2_rows[:, :, first : first + width])
+            for a in range(0, width, UNIT):
+                raw_of[(first + a) // UNIT] = (raw, a)
+            first += width
+            if first == WC1_LOAD_AT:
+                nc.sync.dma_start(out=wc1_rows[:], in_=Wc1.rearrange("(m t) h -> m t h", t=PACK))
+
+        one = keep.tile([P, 1], F32)
+        nc.vector.memset(one[:], 1.0)
+        warm = keep.tile([P, 1], F32)
+        nc.scalar.activation(out=warm[:], in_=one[:], func=ACT.Sqrt)
+
+        sign = keep.tile([P, PACK], F32)
+        nc.vector.tensor_scalar(out=sign[:], in0=prm[:, 0, 0:PACK], scalar1=0.0, scalar2=2.0, op0=ALU.is_ge, op1=ALU.mult)
+        nc.vector.tensor_scalar(out=sign[:], in0=sign[:], scalar1=-1.0, scalar2=None, op0=ALU.add)
+
+        var_eps, std, rough, newton, rstd, gain, shift = {}, {}, {}, {}, {}, {}, {}
+        for k in range(2):
+            var_eps[k] = keep.tile([P, PACK], F32, name="var_eps%d" % k)
+            std[k] = keep.tile([P, PACK], F32, name="std%d" % k)
+            rough[k] = keep.tile([P, PACK], F32, name="rough%d" % k)
+            newton[k] = keep.tile([P, PACK], F32, name="newton%d" % k)
+            rstd[k] = keep.tile([P, PACK], F32, name="rstd%d" % k)
+            gain[k] = keep.tile([P, PACK], F32, name="gain%d" % k)
+            shift[k] = keep.tile([P, PACK], F32, name="shift%d" % k)
+        gain_abs = keep.tile([P, PACK], F32)
+
+        def norm_root(k):
+            nc.gpsimd.tensor_scalar(
+                out=var_eps[k][:], in0=prm[:, 6 + k, 0:PACK], scalar1=1.0, scalar2=BN_EPS, op0=ALU.mult, op1=ALU.add
+            )
+            nc.scalar.activation(out=std[k][:], in_=var_eps[k][:], func=ACT.Sqrt)
+
+        def norm_reciprocal(k):
+            nc.vector.reciprocal(out=rough[k][:], in_=std[k][:])
+
+        def norm_gain_shift(k):
+            tt = nc.gpsimd.tensor_tensor
+            tt(out=newton[k][:], in0=rough[k][:], in1=rough[k][:], op=ALU.mult)
+            tt(out=newton[k][:], in0=newton[k][:], in1=var_eps[k][:], op=ALU.mult)
+            nc.gpsimd.tensor_scalar(out=newton[k][:], in0=newton[k][:], scalar1=-0.5, scalar2=1.5, op0=ALU.mult, op1=ALU.add)
+            tt(out=rstd[k][:], in0=rough[k][:], in1=newton[k][:], op=ALU.mult)
+            tt(out=gain[k][:], in0=prm[:, k, 0:PACK], in1=rstd[k][:], op=ALU.mult)
+            tt(out=shift[k][:], in0=prm[:, 4 + k, 0:PACK], in1=gain[k][:], op=ALU.mult)
+            tt(out=shift[k][:], in0=prm[:, 2 + k, 0:PACK], in1=shift[k][:], op=ALU.subtract)
+
+        norm_root(0)
+        norm_reciprocal(0)
+        norm_gain_shift(0)
+        nc.gpsimd.tensor_tensor(out=gain_abs[:], in0=gain[0][:], in1=sign[:], op=ALU.mult)
+
+        w3_signed = keep.tile([P, PACK, H], BF16)
+        for t in range(PACK):
+            nc.vector.tensor_scalar(
+                out=w3_signed[:, t, :], in0=w3_rows[:, t, :], scalar1=sign[:, t : t + 1], scalar2=None, op0=ALU.mult
+            )
+
+        def turn_weights(rows):
+            halves = []
+            for b in range(2):
+                turned = psum.tile([P, 2, 2, P], F32, tag="aux", bufs=2)
+                for i in range(2):
+                    words = rows[:, 2 * b + i, :].bitcast(F32)
+                    for u in range(2):
+                        nc.tensor.transpose(turned[:, i, u, :], words[:, u : H // 2 : 2], ident[:])
+                halves.append(turned)
+            return halves
+
+        def group_weights(halves, copy):
+            grouped_w = keep.tile([P, PACK * H], BF16, align_bytes=64)
+            words_out = grouped_w[:].bitcast(F32).rearrange("p (t m u) -> p t m u", t=PACK, u=2)
+            for b in range(2):
+                copy(out=words_out[:, 2 * b : 2 * b + 2, :, :], in_=halves[b][:].rearrange("p t u m -> p t m u"))
+            return grouped_w
+
+        def quantize_weights(grouped_w, codes, scales):
+            nc.vector.quantize_mx(out=codes[:].bitcast(FP8X4), scales=scales[:], in_=grouped_w[:])
+
+        w3_codes = keep.tile([P, H], U32, align_bytes=64)
+        w3_scales = keep.tile([P, H], U8, align_bytes=64)
+        wc1_codes = keep.tile([P, H], U32, align_bytes=64)
+        wc1_scales = keep.tile([P, H], U8, align_bytes=64)
+        w3_grouped = group_weights(turn_weights(w3_signed), nc.vector.tensor_copy)
+
+        grouped_of = {}
+        codes_of = {}
+        bank_of = {}
+
+        def rows_of(u):
+            raw, a = raw_of[u]
+            return raw[:, :, a : a + UNIT].rearrange("p j c -> p c j")
+
+        def interleave_most(u):
+            grouped = grpp.tile([P, UNIT, PACK], BF16, tag="grouped", align_bytes=64)
+            nc.scalar.copy(out=grouped[:, 0:S_COLS, :], in_=rows_of(u)[:, 0:S_COLS, :])
+            grouped_of[u] = grouped
+
+        def interleave_rest(u):
+            if u < GROUPED_BUFS:
+                nc.vector.tensor_copy(out=grouped_of[u][:, S_COLS:UNIT, :], in_=rows_of(u)[:, S_COLS:UNIT, :])
+            else:
+                nc.gpsimd.tensor_scalar(
+                    out=grouped_of[u][:, S_COLS:UNIT, :],
+                    in0=rows_of(u)[:, S_COLS:UNIT, :],
+                    scalar1=1.0,
+                    scalar2=0.0,
+                    op0=ALU.mult,
+                    op1=ALU.add,
+                )
+
+        def interleave(u):
+            interleave_most(u)
+            interleave_rest(u)
+
+        def quantize(u):
+            codes = codp.tile([P, UNIT], U32, tag="codes", align_bytes=64)
+            scales = codp.tile([P, UNIT], U8, tag="scales", align_bytes=64)
+            nc.vector.quantize_mx(
+                out=codes[:].bitcast(FP8X4), scales=scales[:], in_=grouped_of[u][:].rearrange("p c j -> p (c j)")
+            )
+            codes_of[u] = (codes, scales)
+
+        def multiply(s):
+            u, t = divmod(s, PACK)
+            codes, scales = codes_of[u]
+            bank = psum.tile([P, UNIT], BF16, tag="x3")
+            nc.tensor.matmul_mx(
+                out=bank[:],
+                lhsT=w3_codes[:, t * P : (t + 1) * P].bitcast(FP8X4),
+                lhsT_scale=w3_scales[:, t * P : (t + 1) * P],
+                rhs=codes[:].bitcast(FP8X4),
+                rhs_scale=scales[:],
+                start=True,
+                stop=True,
+            )
+            bank_of[s] = bank
+
+        top = keep.tile([P, PACK, UNIT], BF16)
+
+        def read_bank(s):
+            t = s % PACK
+            if s < PACK:
+                nc.vector.tensor_copy(out=top[:, t, :], in_=bank_of[s][:])
+            else:
+                nc.vector.tensor_tensor(out=top[:, t, :], in0=bank_of[s][:], in1=top[:, t, :], op=ALU.max)
+
+        for u in range(GROUPED_BUFS):
+            interleave_most(u)
+        interleave_rest(0)
+        quantize_weights(w3_grouped, w3_codes, w3_scales)
+        quantize(0)
+        interleave(GROUPED_BUFS)
+        for s in range(PACK):
+            multiply(s)
+        interleave_rest(1)
+        quantize(1)
+        interleave(GROUPED_BUFS + 1)
+        for s in range(PACK, AHEAD):
+            multiply(s)
+
+        for s in range(BANKS):
+            nxt = s + AHEAD
+            if nxt < BANKS and nxt % PACK == 0:
+                quantize(nxt // PACK)
+                if nxt // PACK + GROUPED_BUFS < UNITS:
+                    interleave(nxt // PACK + GROUPED_BUFS)
+            read_bank(s)
+            if nxt < BANKS:
+                multiply(nxt)
+            if s == WC1_AT:
+                wc1_halves = turn_weights(wc1_rows)
+                norm_root(1)
+            if s == WC1_AT + 2 * PACK:
+                wc1_grouped = group_weights(wc1_halves, nc.scalar.copy)
+                norm_reciprocal(1)
+            if s == WC1_AT + 5 * PACK:
+                quantize_weights(wc1_grouped, wc1_codes, wc1_scales)
+        norm_gain_shift(1)
+
+        half = keep.tile([P, PACK, 2 * NPTS], BF16)
+        peak = keep.tile([P, PACK, NPTS], BF16)
+        pooled = keep.tile([P, PACK, NPTS], BF16)
+        for t in (0, 2):
+            nc.vector.tensor_tensor(
+                out=half[:, t : t + 2, :], in0=top[:, t : t + 2, 0 : 2 * NPTS], in1=top[:, t : t + 2, 2 * NPTS : UNIT], op=ALU.max
+            )
+        for t in (0, 2):
+            nc.vector.tensor_tensor(
+                out=peak[:, t : t + 2, :], in0=half[:, t : t + 2, 0:NPTS], in1=half[:, t : t + 2, NPTS : 2 * NPTS], op=ALU.max
+            )
+        for t in range(PACK):
+            nc.scalar.activation(
+                out=pooled[:, t, :], in_=peak[:, t, :], func=ACT.Relu, bias=shift[0][:, t : t + 1], scale=gain_abs[:, t : t + 1]
+            )
+
+        p_grouped = keep.tile([P, NPTS, PACK], BF16, align_bytes=64)
+        nc.vector.tensor_copy(out=p_grouped[:], in_=pooled[:].rearrange("p t n -> p n t"))
+        p_codes = keep.tile([P, NPTS], U32, align_bytes=64)
+        p_scales = keep.tile([P, NPTS], U8, align_bytes=64)
+        nc.vector.quantize_mx(
+            out=p_codes[:].bitcast(FP8X4), scales=p_scales[:], in_=p_grouped[:].rearrange("p n t -> p (n t)")
+        )
+        xc = psum.tile([P, PACK, NPTS], F32, tag="aux", bufs=2)
+        for t in range(PACK):
+            nc.tensor.matmul_mx(
+                out=xc[:, t, :],
+                lhsT=wc1_codes[:, t * P : (t + 1) * P].bitcast(FP8X4),
+                lhsT_scale=wc1_scales[:, t * P : (t + 1) * P],
+                rhs=p_codes[:].bitcast(FP8X4),
+                rhs_scale=p_scales[:],
+                start=True,
+                stop=True,
+            )
+        result = keep.tile([P, PACK, NPTS], F32)
+        for t in range(PACK):
+            nc.scalar.activation(
+                out=result[:, t, :], in_=xc[:, t, :], func=ACT.Relu, bias=shift[1][:, t : t + 1], scale=gain[1][:, t : t + 1]
+            )
+        nc.sync.dma_start(out=out[0].rearrange("(m t) n -> m t n", t=PACK), in_=result[:])

@@ -23,10 +23,11 @@ LOADS = (UNIT,) * SHORT_LOADS + (2 * UNIT,) * ((UNITS - SHORT_LOADS) // 2)
 WC1_LOAD_AT = 12 * UNIT
 BANKS = UNITS * PACK
 AHEAD = 6
+READ_ORDER = (3, 0, 1, 2)
 GROUPED_BUFS = 2
-S_COLS = 336
+S_COLS = 352
 BN_EPS = 1e-5
-WC1_AT = 48
+NORM2_AT = 10
 
 FLOPS = 2 * H * H * (COLS + NPTS)
 
@@ -213,37 +214,42 @@ def tile_p2b_xcorr_pb_kernel(tc, h2, W3, g3, b3, m3, v3, Wc1, gc1, bc1, mc1, vc1
             else:
                 nc.vector.tensor_tensor(out=top[:, t, :], in0=bank_of[s][:], in1=top[:, t, :], op=ALU.max)
 
+        was_read = set()
+        issued = []
+
+        def refill():
+            while len(issued) < BANKS and len(issued) // PACK in codes_of and (len(issued) < AHEAD or len(issued) - AHEAD in was_read):
+                multiply(len(issued))
+                issued.append(len(issued))
+
+
         for u in range(GROUPED_BUFS):
             interleave_most(u)
         interleave_rest(0)
         quantize_weights(w3_grouped, w3_codes, w3_scales)
         quantize(0)
         interleave(GROUPED_BUFS)
-        for s in range(PACK):
-            multiply(s)
+        refill()
         interleave_rest(1)
         quantize(1)
         interleave(GROUPED_BUFS + 1)
-        for s in range(PACK, AHEAD):
-            multiply(s)
+        refill()
 
-        for s in range(BANKS):
-            nxt = s + AHEAD
-            if nxt < BANKS and nxt % PACK == 0:
-                quantize(nxt // PACK)
-                if nxt // PACK + GROUPED_BUFS < UNITS:
-                    interleave(nxt // PACK + GROUPED_BUFS)
-            read_bank(s)
-            if nxt < BANKS:
-                multiply(nxt)
-            if s == WC1_AT:
-                wc1_halves = turn_weights(wc1_rows)
+        for r in range(UNITS):
+            if r + 2 < UNITS:
+                quantize(r + 2)
+                if r + 2 + GROUPED_BUFS < UNITS:
+                    interleave(r + 2 + GROUPED_BUFS)
+            for t in READ_ORDER:
+                read_bank(r * PACK + t)
+                was_read.add(r * PACK + t)
+                refill()
+            if r == NORM2_AT:
                 norm_root(1)
-            if s == WC1_AT + 2 * PACK:
-                wc1_grouped = group_weights(wc1_halves, nc.scalar.copy)
+            if r == NORM2_AT + 2:
                 norm_reciprocal(1)
-            if s == WC1_AT + 5 * PACK:
-                quantize_weights(wc1_grouped, wc1_codes, wc1_scales)
+            if r == UNITS - 2:
+                wc1_grouped = group_weights(turn_weights(wc1_rows), nc.scalar.copy)
         norm_gain_shift(1)
 
         half = keep.tile([P, PACK, 2 * NPTS], BF16)
@@ -261,6 +267,7 @@ def tile_p2b_xcorr_pb_kernel(tc, h2, W3, g3, b3, m3, v3, Wc1, gc1, bc1, mc1, vc1
             nc.scalar.activation(
                 out=pooled[:, t, :], in_=peak[:, t, :], func=ACT.Relu, bias=shift[0][:, t : t + 1], scale=gain_abs[:, t : t + 1]
             )
+        quantize_weights(wc1_grouped, wc1_codes, wc1_scales)
 
         p_grouped = keep.tile([P, NPTS, PACK], BF16, align_bytes=64)
         nc.vector.tensor_copy(out=p_grouped[:], in_=pooled[:].rearrange("p t n -> p n t"))

@@ -27,7 +27,7 @@ READ_ORDER = (3, 0, 1, 2)
 GROUPED_BUFS = 2
 S_COLS = 352
 BN_EPS = 1e-5
-NORM2_AT = 10
+NORM2_AT = 16
 
 FLOPS = 2 * H * H * (COLS + NPTS)
 
@@ -54,10 +54,6 @@ def tile_p2b_xcorr_pb_kernel(tc, h2, W3, g3, b3, m3, v3, Wc1, gc1, bc1, mc1, vc1
 
         ident = keep.tile([P, P], F32)
         make_identity(nc, ident[:])
-        load_vector(nc.gpsimd, 7, vc1)
-        load_vector(nc.gpsimd, 1, gc1)
-        load_vector(nc.gpsimd, 3, bc1)
-        load_vector(nc.gpsimd, 5, mc1)
 
         w3_rows = keep.tile([P, PACK, H], BF16)
         nc.sync.dma_start(out=w3_rows[:], in_=W3.rearrange("(m t) h -> m t h", t=PACK))
@@ -74,6 +70,10 @@ def tile_p2b_xcorr_pb_kernel(tc, h2, W3, g3, b3, m3, v3, Wc1, gc1, bc1, mc1, vc1
             first += width
             if first == WC1_LOAD_AT:
                 nc.sync.dma_start(out=wc1_rows[:], in_=Wc1.rearrange("(m t) h -> m t h", t=PACK))
+                load_vector(nc.sync, 7, vc1)
+                load_vector(nc.sync, 1, gc1)
+                load_vector(nc.sync, 3, bc1)
+                load_vector(nc.sync, 5, mc1)
 
         one = keep.tile([P, 1], F32)
         nc.vector.memset(one[:], 1.0)
@@ -230,16 +230,16 @@ def tile_p2b_xcorr_pb_kernel(tc, h2, W3, g3, b3, m3, v3, Wc1, gc1, bc1, mc1, vc1
         quantize(0)
         interleave(GROUPED_BUFS)
         refill()
-        interleave_rest(1)
-        quantize(1)
-        interleave(GROUPED_BUFS + 1)
-        refill()
 
         for r in range(UNITS):
-            if r + 2 < UNITS:
-                quantize(r + 2)
-                if r + 2 + GROUPED_BUFS < UNITS:
-                    interleave(r + 2 + GROUPED_BUFS)
+            nxt = r + 1
+            if nxt < UNITS:
+                if nxt < GROUPED_BUFS:
+                    interleave_rest(nxt)
+                quantize(nxt)
+                if nxt + GROUPED_BUFS < UNITS:
+                    interleave(nxt + GROUPED_BUFS)
+                refill()
             for t in READ_ORDER:
                 read_bank(r * PACK + t)
                 was_read.add(r * PACK + t)

@@ -48,15 +48,14 @@ def tile_p2b_xcorr_pb_kernel(tc, h2, W3, g3, b3, m3, v3, Wc1, gc1, bc1, mc1, vc1
             queue.dma_start(out=prm[:, slot, 0:PACK], in_=vec.rearrange("(p t) -> p t", t=PACK))
 
         load_vector(nc.scalar, 0, g3)
-        load_vector(nc.scalar, 6, v3)
-        load_vector(nc.scalar, 2, b3)
-        load_vector(nc.scalar, 4, m3)
 
         ident = keep.tile([P, P], F32)
         make_identity(nc, ident[:])
 
-        w3_rows = keep.tile([P, PACK, H], BF16)
-        nc.sync.dma_start(out=w3_rows[:], in_=W3.rearrange("(m t) h -> m t h", t=PACK))
+        w3_rows = {}
+        for b in range(2):
+            w3_rows[b] = keep.tile([P, 2, H], BF16, name="w3_rows%d" % b)
+            nc.sync.dma_start(out=w3_rows[b][:], in_=W3.rearrange("(m t) h -> m t h", t=PACK)[:, 2 * b : 2 * b + 2, :])
         wc1_rows = keep.tile([P, PACK, H], BF16)
 
         h2_rows = h2[0].rearrange("(p j) m n -> p j (m n)", j=PACK)
@@ -70,7 +69,10 @@ def tile_p2b_xcorr_pb_kernel(tc, h2, W3, g3, b3, m3, v3, Wc1, gc1, bc1, mc1, vc1
             first += width
             if first == WC1_LOAD_AT:
                 nc.sync.dma_start(out=wc1_rows[:], in_=Wc1.rearrange("(m t) h -> m t h", t=PACK))
+                load_vector(nc.sync, 6, v3)
                 load_vector(nc.sync, 7, vc1)
+                load_vector(nc.sync, 2, b3)
+                load_vector(nc.sync, 4, m3)
                 load_vector(nc.sync, 1, gc1)
                 load_vector(nc.sync, 3, bc1)
                 load_vector(nc.sync, 5, mc1)
@@ -114,15 +116,10 @@ def tile_p2b_xcorr_pb_kernel(tc, h2, W3, g3, b3, m3, v3, Wc1, gc1, bc1, mc1, vc1
             tt(out=shift[k][:], in0=prm[:, 4 + k, 0:PACK], in1=gain[k][:], op=ALU.mult)
             tt(out=shift[k][:], in0=prm[:, 2 + k, 0:PACK], in1=shift[k][:], op=ALU.subtract)
 
-        norm_root(0)
-        norm_reciprocal(0)
-        norm_gain_shift(0)
-        nc.gpsimd.tensor_tensor(out=gain_abs[:], in0=gain[0][:], in1=sign[:], op=ALU.mult)
-
         w3_signed = keep.tile([P, PACK, H], BF16)
         for t in range(PACK):
             nc.vector.tensor_scalar(
-                out=w3_signed[:, t, :], in0=w3_rows[:, t, :], scalar1=sign[:, t : t + 1], scalar2=None, op0=ALU.mult
+                out=w3_signed[:, t, :], in0=w3_rows[t // 2][:, t % 2, :], scalar1=sign[:, t : t + 1], scalar2=None, op0=ALU.mult
             )
 
         def turn_weights(rows):
@@ -166,17 +163,14 @@ def tile_p2b_xcorr_pb_kernel(tc, h2, W3, g3, b3, m3, v3, Wc1, gc1, bc1, mc1, vc1
             grouped_of[u] = grouped
 
         def interleave_rest(u):
-            if u < GROUPED_BUFS:
-                nc.vector.tensor_copy(out=grouped_of[u][:, S_COLS:UNIT, :], in_=rows_of(u)[:, S_COLS:UNIT, :])
-            else:
-                nc.gpsimd.tensor_scalar(
-                    out=grouped_of[u][:, S_COLS:UNIT, :],
-                    in0=rows_of(u)[:, S_COLS:UNIT, :],
-                    scalar1=1.0,
-                    scalar2=0.0,
-                    op0=ALU.mult,
-                    op1=ALU.add,
-                )
+            nc.gpsimd.tensor_scalar(
+                out=grouped_of[u][:, S_COLS:UNIT, :],
+                in0=rows_of(u)[:, S_COLS:UNIT, :],
+                scalar1=1.0,
+                scalar2=0.0,
+                op0=ALU.mult,
+                op1=ALU.add,
+            )
 
         def interleave(u):
             interleave_most(u)
@@ -224,8 +218,7 @@ def tile_p2b_xcorr_pb_kernel(tc, h2, W3, g3, b3, m3, v3, Wc1, gc1, bc1, mc1, vc1
 
 
         for u in range(GROUPED_BUFS):
-            interleave_most(u)
-        interleave_rest(0)
+            interleave(u)
         quantize_weights(w3_grouped, w3_codes, w3_scales)
         quantize(0)
         interleave(GROUPED_BUFS)
@@ -234,8 +227,6 @@ def tile_p2b_xcorr_pb_kernel(tc, h2, W3, g3, b3, m3, v3, Wc1, gc1, bc1, mc1, vc1
         for r in range(UNITS):
             nxt = r + 1
             if nxt < UNITS:
-                if nxt < GROUPED_BUFS:
-                    interleave_rest(nxt)
                 quantize(nxt)
                 if nxt + GROUPED_BUFS < UNITS:
                     interleave(nxt + GROUPED_BUFS)
@@ -245,12 +236,17 @@ def tile_p2b_xcorr_pb_kernel(tc, h2, W3, g3, b3, m3, v3, Wc1, gc1, bc1, mc1, vc1
                 was_read.add(r * PACK + t)
                 refill()
             if r == NORM2_AT:
+                norm_root(0)
                 norm_root(1)
             if r == NORM2_AT + 2:
+                norm_reciprocal(0)
                 norm_reciprocal(1)
+            if r == UNITS - GROUPED_BUFS - 2:
+                norm_gain_shift(0)
+                nc.gpsimd.tensor_tensor(out=gain_abs[:], in0=gain[0][:], in1=sign[:], op=ALU.mult)
+                norm_gain_shift(1)
             if r == UNITS - 2:
                 wc1_grouped = group_weights(turn_weights(wc1_rows), nc.scalar.copy)
-        norm_gain_shift(1)
 
         half = keep.tile([P, PACK, 2 * NPTS], BF16)
         peak = keep.tile([P, PACK, NPTS], BF16)
@@ -276,10 +272,11 @@ def tile_p2b_xcorr_pb_kernel(tc, h2, W3, g3, b3, m3, v3, Wc1, gc1, bc1, mc1, vc1
         nc.vector.quantize_mx(
             out=p_codes[:].bitcast(FP8X4), scales=p_scales[:], in_=p_grouped[:].rearrange("p n t -> p (n t)")
         )
-        xc = psum.tile([P, PACK, NPTS], F32, tag="aux", bufs=2)
+        xc = {}
         for t in range(PACK):
+            xc[t] = psum.tile([P, NPTS], F32, tag="x3", name="xc%d" % t)
             nc.tensor.matmul_mx(
-                out=xc[:, t, :],
+                out=xc[t][:],
                 lhsT=wc1_codes[:, t * P : (t + 1) * P].bitcast(FP8X4),
                 lhsT_scale=wc1_scales[:, t * P : (t + 1) * P],
                 rhs=p_codes[:].bitcast(FP8X4),
@@ -287,9 +284,12 @@ def tile_p2b_xcorr_pb_kernel(tc, h2, W3, g3, b3, m3, v3, Wc1, gc1, bc1, mc1, vc1
                 start=True,
                 stop=True,
             )
-        result = keep.tile([P, PACK, NPTS], F32)
-        for t in range(PACK):
-            nc.scalar.activation(
-                out=result[:, t, :], in_=xc[:, t, :], func=ACT.Relu, bias=shift[1][:, t : t + 1], scale=gain[1][:, t : t + 1]
-            )
-        nc.sync.dma_start(out=out[0].rearrange("(m t) n -> m t n", t=PACK), in_=result[:])
+        out_rows = out[0].rearrange("(m t) n -> m t n", t=PACK)
+        for b in range(2):
+            result = keep.tile([P, 2, NPTS], F32, name="result%d" % b)
+            for i in range(2):
+                t = 2 * b + i
+                nc.scalar.activation(
+                    out=result[:, i, :], in_=xc[t][:], func=ACT.Relu, bias=shift[1][:, t : t + 1], scale=gain[1][:, t : t + 1]
+                )
+            nc.sync.dma_start(out=out_rows[:, 2 * b : 2 * b + 2, :], in_=result[:])

@@ -24,7 +24,10 @@ WC1_LOAD_AT = 12 * UNIT
 BANKS = UNITS * PACK
 AHEAD = 6
 READ_ORDER = (3, 0, 1, 2)
-GROUPED_BUFS = 2
+LATER_ORDER = (0, 1, 3, 2)
+SINGLE = 4
+ROUNDS = tuple((u,) for u in range(SINGLE)) + tuple((u, u + 1) for u in range(SINGLE, UNITS, 2))
+GROUPED_BUFS = 4
 S_COLS = 352
 BN_EPS = 1e-5
 NORM2_AT = 16
@@ -217,36 +220,39 @@ def tile_p2b_xcorr_pb_kernel(tc, h2, W3, g3, b3, m3, v3, Wc1, gc1, bc1, mc1, vc1
                 issued.append(len(issued))
 
 
-        for u in range(GROUPED_BUFS):
-            interleave(u)
-        quantize_weights(w3_grouped, w3_codes, w3_scales)
-        quantize(0)
-        interleave(GROUPED_BUFS)
-        refill()
-
-        for r in range(UNITS):
-            nxt = r + 1
-            if nxt < UNITS:
-                quantize(nxt)
-                if nxt + GROUPED_BUFS < UNITS:
-                    interleave(nxt + GROUPED_BUFS)
-                refill()
-            for t in READ_ORDER:
-                read_bank(r * PACK + t)
-                was_read.add(r * PACK + t)
-                refill()
-            if r == NORM2_AT:
-                norm_root(0)
-                norm_root(1)
-            if r == NORM2_AT + 2:
-                norm_reciprocal(0)
-                norm_reciprocal(1)
-            if r == UNITS - GROUPED_BUFS - 2:
+        def prepare(u):
+            quantize(u)
+            if u + GROUPED_BUFS < UNITS:
+                interleave(u + GROUPED_BUFS)
+            if u + GROUPED_BUFS == UNITS - 1:
                 norm_gain_shift(0)
                 nc.gpsimd.tensor_tensor(out=gain_abs[:], in0=gain[0][:], in1=sign[:], op=ALU.mult)
                 norm_gain_shift(1)
-            if r == UNITS - 2:
-                wc1_grouped = group_weights(turn_weights(wc1_rows), nc.scalar.copy)
+            refill()
+
+        for u in range(GROUPED_BUFS):
+            interleave(u)
+        quantize_weights(w3_grouped, w3_codes, w3_scales)
+        for u in ROUNDS[0]:
+            prepare(u)
+
+        for i in range(len(ROUNDS)):
+            if i + 1 < len(ROUNDS):
+                for u in ROUNDS[i + 1]:
+                    prepare(u)
+            for r in ROUNDS[i]:
+                for t in range(PACK) if r in (0, UNITS - 1) else READ_ORDER if r == ROUNDS[i][0] else LATER_ORDER:
+                    read_bank(r * PACK + t)
+                    was_read.add(r * PACK + t)
+                    refill()
+                if r == NORM2_AT:
+                    norm_root(0)
+                    norm_root(1)
+                if r == NORM2_AT + 2:
+                    norm_reciprocal(0)
+                    norm_reciprocal(1)
+                if r == UNITS - 2:
+                    wc1_grouped = group_weights(turn_weights(wc1_rows), nc.scalar.copy)
 
         half = keep.tile([P, PACK, 2 * NPTS], BF16)
         peak = keep.tile([P, PACK, NPTS], BF16)

@@ -28,6 +28,9 @@ LATER_ORDER = (0, 1, 3, 2)
 SINGLE = 4
 ROUNDS = tuple((u,) for u in range(SINGLE)) + tuple((u, u + 1) for u in range(SINGLE, UNITS, 2))
 GROUPED_BUFS = 4
+WARM_FIRST = 8
+WARM_SECOND = 5
+WARM_LAST = 3
 S_COLS = 352
 BN_EPS = 1e-5
 NORM2_AT = 16
@@ -54,6 +57,16 @@ def tile_p2b_xcorr_pb_kernel(tc, h2, W3, g3, b3, m3, v3, Wc1, gc1, bc1, mc1, vc1
 
         ident = keep.tile([P, P], F32)
         make_identity(nc, ident[:])
+
+        zeros = keep.tile([P, UNIT], BF16)
+        nc.vector.memset(zeros[:], 0.0)
+
+        def keep_warm(passes):
+            idle = psum.tile([P, UNIT], F32, tag="aux", bufs=2)
+            for i in range(passes):
+                nc.tensor.matmul(out=idle[:], lhsT=zeros[:, 0:P], rhs=zeros[:], start=True, stop=True)
+
+        keep_warm(WARM_FIRST)
 
         w3_rows = {}
         for b in range(2):
@@ -151,6 +164,7 @@ def tile_p2b_xcorr_pb_kernel(tc, h2, W3, g3, b3, m3, v3, Wc1, gc1, bc1, mc1, vc1
         wc1_codes = keep.tile([P, H], U32, align_bytes=64)
         wc1_scales = keep.tile([P, H], U8, align_bytes=64)
         w3_grouped = group_weights(turn_weights(w3_signed), nc.vector.tensor_copy)
+        keep_warm(WARM_SECOND)
 
         grouped_of = {}
         codes_of = {}
@@ -253,6 +267,7 @@ def tile_p2b_xcorr_pb_kernel(tc, h2, W3, g3, b3, m3, v3, Wc1, gc1, bc1, mc1, vc1
                     norm_reciprocal(1)
                 if r == UNITS - 2:
                     wc1_grouped = group_weights(turn_weights(wc1_rows), nc.scalar.copy)
+                    keep_warm(WARM_LAST)
 
         half = keep.tile([P, PACK, 2 * NPTS], BF16)
         peak = keep.tile([P, PACK, NPTS], BF16)

@@ -28,6 +28,8 @@ LATER_ORDER = (0, 1, 3, 2)
 SINGLE = 4
 ROUNDS = tuple((u,) for u in range(SINGLE)) + tuple((u, u + 1) for u in range(SINGLE, UNITS, 2))
 GROUPED_BUFS = 4
+EARLY = 4
+S_COLS_EARLY = 288
 WARM_FIRST = 8
 WARM_SECOND = 5
 WARM_LAST = 3
@@ -149,11 +151,13 @@ def tile_p2b_xcorr_pb_kernel(tc, h2, W3, g3, b3, m3, v3, Wc1, gc1, bc1, mc1, vc1
                 halves.append(turned)
             return halves
 
-        def group_weights(halves, copy):
+        def group_weights(halves, copy, then=None):
             grouped_w = keep.tile([P, PACK * H], BF16, align_bytes=64)
             words_out = grouped_w[:].bitcast(F32).rearrange("p (t m u) -> p t m u", t=PACK, u=2)
             for b in range(2):
                 copy(out=words_out[:, 2 * b : 2 * b + 2, :, :], in_=halves[b][:].rearrange("p t u m -> p t m u"))
+                if then is not None:
+                    then(grouped_w, b)
             return grouped_w
 
         def quantize_weights(grouped_w, codes, scales):
@@ -163,7 +167,15 @@ def tile_p2b_xcorr_pb_kernel(tc, h2, W3, g3, b3, m3, v3, Wc1, gc1, bc1, mc1, vc1
         w3_scales = keep.tile([P, H], U8, align_bytes=64)
         wc1_codes = keep.tile([P, H], U32, align_bytes=64)
         wc1_scales = keep.tile([P, H], U8, align_bytes=64)
-        w3_grouped = group_weights(turn_weights(w3_signed), nc.vector.tensor_copy)
+
+        def quantize_w3_half(grouped_w, b):
+            nc.vector.quantize_mx(
+                out=w3_codes[:, b * H // 2 : (b + 1) * H // 2].bitcast(FP8X4),
+                scales=w3_scales[:, b * H // 2 : (b + 1) * H // 2],
+                in_=grouped_w[:, b * PACK * H // 2 : (b + 1) * PACK * H // 2],
+            )
+
+        group_weights(turn_weights(w3_signed), nc.vector.tensor_copy, quantize_w3_half)
         keep_warm(WARM_SECOND)
 
         grouped_of = {}
@@ -174,15 +186,18 @@ def tile_p2b_xcorr_pb_kernel(tc, h2, W3, g3, b3, m3, v3, Wc1, gc1, bc1, mc1, vc1
             raw, a = raw_of[u]
             return raw[:, :, a : a + UNIT].rearrange("p j c -> p c j")
 
+        def s_end(u):
+            return S_COLS_EARLY if u < EARLY else S_COLS
+
         def interleave_most(u):
             grouped = grpp.tile([P, UNIT, PACK], BF16, tag="grouped", align_bytes=64)
-            nc.scalar.copy(out=grouped[:, 0:S_COLS, :], in_=rows_of(u)[:, 0:S_COLS, :])
+            nc.scalar.copy(out=grouped[:, 0 : s_end(u), :], in_=rows_of(u)[:, 0 : s_end(u), :])
             grouped_of[u] = grouped
 
         def interleave_rest(u):
             nc.gpsimd.tensor_scalar(
-                out=grouped_of[u][:, S_COLS:UNIT, :],
-                in0=rows_of(u)[:, S_COLS:UNIT, :],
+                out=grouped_of[u][:, s_end(u) : UNIT, :],
+                in0=rows_of(u)[:, s_end(u) : UNIT, :],
                 scalar1=1.0,
                 scalar2=0.0,
                 op0=ALU.mult,
@@ -216,14 +231,17 @@ def tile_p2b_xcorr_pb_kernel(tc, h2, W3, g3, b3, m3, v3, Wc1, gc1, bc1, mc1, vc1
             )
             bank_of[s] = bank
 
-        top = keep.tile([P, PACK, UNIT], BF16)
+        tops = {}
+        for k in range(2):
+            tops[k] = keep.tile([P, PACK, UNIT], BF16, name="top%d" % k)
+        top = tops[UNITS % 2]
 
         def read_bank(s):
-            t = s % PACK
-            if s < PACK:
-                nc.vector.tensor_copy(out=top[:, t, :], in_=bank_of[s][:])
+            u, t = divmod(s, PACK)
+            if u == 0:
+                nc.vector.tensor_copy(out=tops[1][:, t, :], in_=bank_of[s][:])
             else:
-                nc.vector.tensor_tensor(out=top[:, t, :], in0=bank_of[s][:], in1=top[:, t, :], op=ALU.max)
+                nc.vector.tensor_tensor(out=tops[(u + 1) % 2][:, t, :], in0=bank_of[s][:], in1=tops[u % 2][:, t, :], op=ALU.max)
 
         was_read = set()
         issued = []
@@ -246,7 +264,6 @@ def tile_p2b_xcorr_pb_kernel(tc, h2, W3, g3, b3, m3, v3, Wc1, gc1, bc1, mc1, vc1
 
         for u in range(GROUPED_BUFS):
             interleave(u)
-        quantize_weights(w3_grouped, w3_codes, w3_scales)
         for u in ROUNDS[0]:
             prepare(u)
 
@@ -271,7 +288,7 @@ def tile_p2b_xcorr_pb_kernel(tc, h2, W3, g3, b3, m3, v3, Wc1, gc1, bc1, mc1, vc1
 
         half = keep.tile([P, PACK, 2 * NPTS], BF16)
         peak = keep.tile([P, PACK, NPTS], BF16)
-        pooled = keep.tile([P, PACK, NPTS], BF16)
+        linear = keep.tile([P, PACK, NPTS], F32)
         for t in (0, 2):
             nc.vector.tensor_tensor(
                 out=half[:, t : t + 2, :], in0=top[:, t : t + 2, 0 : 2 * NPTS], in1=top[:, t : t + 2, 2 * NPTS : UNIT], op=ALU.max
@@ -281,13 +298,26 @@ def tile_p2b_xcorr_pb_kernel(tc, h2, W3, g3, b3, m3, v3, Wc1, gc1, bc1, mc1, vc1
                 out=peak[:, t : t + 2, :], in0=half[:, t : t + 2, 0:NPTS], in1=half[:, t : t + 2, NPTS : 2 * NPTS], op=ALU.max
             )
         for t in range(PACK):
-            nc.scalar.activation(
-                out=pooled[:, t, :], in_=peak[:, t, :], func=ACT.Relu, bias=shift[0][:, t : t + 1], scale=gain_abs[:, t : t + 1]
+            nc.vector.tensor_scalar(
+                out=linear[:, t, :],
+                in0=peak[:, t, :],
+                scalar1=gain_abs[:, t : t + 1],
+                scalar2=shift[0][:, t : t + 1],
+                op0=ALU.mult,
+                op1=ALU.add,
             )
-        quantize_weights(wc1_grouped, wc1_codes, wc1_scales)
 
+        def quantize_wc1_half(b):
+            nc.vector.quantize_mx(
+                out=wc1_codes[:, b * H // 2 : (b + 1) * H // 2].bitcast(FP8X4),
+                scales=wc1_scales[:, b * H // 2 : (b + 1) * H // 2],
+                in_=wc1_grouped[:, b * PACK * H // 2 : (b + 1) * PACK * H // 2],
+            )
+
+        quantize_wc1_half(0)
         p_grouped = keep.tile([P, NPTS, PACK], BF16, align_bytes=64)
-        nc.vector.tensor_copy(out=p_grouped[:], in_=pooled[:].rearrange("p t n -> p n t"))
+        nc.vector.tensor_scalar(out=p_grouped[:], in0=linear[:].rearrange("p t n -> p n t"), scalar1=0.0, scalar2=None, op0=ALU.max)
+        quantize_wc1_half(1)
         p_codes = keep.tile([P, NPTS], U32, align_bytes=64)
         p_scales = keep.tile([P, NPTS], U8, align_bytes=64)
         nc.vector.quantize_mx(
@@ -313,4 +343,4 @@ def tile_p2b_xcorr_pb_kernel(tc, h2, W3, g3, b3, m3, v3, Wc1, gc1, bc1, mc1, vc1
                 nc.scalar.activation(
                     out=result[:, i, :], in_=xc[t][:], func=ACT.Relu, bias=shift[1][:, t : t + 1], scale=gain[1][:, t : t + 1]
                 )
-            nc.sync.dma_start(out=out_rows[:, 2 * b : 2 * b + 2, :], in_=result[:])
+            (nc.sync if b == 0 else nc.scalar).dma_start(out=out_rows[:, 2 * b : 2 * b + 2, :], in_=result[:])

@@ -21,10 +21,8 @@ UNITS = COLS // UNIT
 SHORT_LOADS = 6
 LOADS = (UNIT,) * SHORT_LOADS + (2 * UNIT,) * ((UNITS - SHORT_LOADS) // 2)
 WC1_LOAD_AT = 12 * UNIT
-BANKS = UNITS * PACK
+PAIR = 2
 AHEAD = 6
-READ_ORDER = (3, 0, 1, 2)
-LATER_ORDER = (0, 1, 3, 2)
 SINGLE = 4
 ROUNDS = tuple((u,) for u in range(SINGLE)) + tuple((u, u + 1) for u in range(SINGLE, UNITS, 2))
 GROUPED_BUFS = 4
@@ -32,7 +30,7 @@ EARLY = 4
 S_COLS_EARLY = 288
 WARM_FIRST = 8
 WARM_SECOND = 5
-WARM_LAST = 3
+WARM_LAST = 8
 S_COLS = 352
 BN_EPS = 1e-5
 NORM2_AT = 16
@@ -219,9 +217,11 @@ def tile_p2b_xcorr_pb_kernel(tc, h2, W3, g3, b3, m3, v3, Wc1, gc1, bc1, mc1, vc1
         def multiply(s):
             u, t = divmod(s, PACK)
             codes, scales = codes_of[u]
-            bank = psum.tile([P, UNIT], BF16, tag="x3")
+            if t % PAIR == 0:
+                bank = psum.tile([P, PAIR, UNIT], BF16, tag="x3")
+                bank_of[s // PAIR] = bank
             nc.tensor.matmul_mx(
-                out=bank[:],
+                out=bank_of[s // PAIR][:, t % PAIR, :],
                 lhsT=w3_codes[:, t * P : (t + 1) * P].bitcast(FP8X4),
                 lhsT_scale=w3_scales[:, t * P : (t + 1) * P],
                 rhs=codes[:].bitcast(FP8X4),
@@ -229,25 +229,30 @@ def tile_p2b_xcorr_pb_kernel(tc, h2, W3, g3, b3, m3, v3, Wc1, gc1, bc1, mc1, vc1
                 start=True,
                 stop=True,
             )
-            bank_of[s] = bank
 
         tops = {}
         for k in range(2):
             tops[k] = keep.tile([P, PACK, UNIT], BF16, name="top%d" % k)
         top = tops[UNITS % 2]
 
-        def read_bank(s):
-            u, t = divmod(s, PACK)
+        def read_bank(b):
+            u, t = divmod(b * PAIR, PACK)
             if u == 0:
-                nc.vector.tensor_copy(out=tops[1][:, t, :], in_=bank_of[s][:])
+                nc.vector.tensor_copy(out=tops[1][:, t : t + PAIR, :], in_=bank_of[b][:])
             else:
-                nc.vector.tensor_tensor(out=tops[(u + 1) % 2][:, t, :], in0=bank_of[s][:], in1=tops[u % 2][:, t, :], op=ALU.max)
+                nc.vector.tensor_tensor(
+                    out=tops[(u + 1) % 2][:, t : t + PAIR, :], in0=bank_of[b][:], in1=tops[u % 2][:, t : t + PAIR, :], op=ALU.max
+                )
 
         was_read = set()
         issued = []
 
         def refill():
-            while len(issued) < BANKS and len(issued) // PACK in codes_of and (len(issued) < AHEAD or len(issued) - AHEAD in was_read):
+            while (
+                len(issued) < UNITS * PACK
+                and len(issued) // PACK in codes_of
+                and (len(issued) // PAIR < AHEAD or len(issued) // PAIR - AHEAD in was_read)
+            ):
                 multiply(len(issued))
                 issued.append(len(issued))
 
@@ -272,9 +277,9 @@ def tile_p2b_xcorr_pb_kernel(tc, h2, W3, g3, b3, m3, v3, Wc1, gc1, bc1, mc1, vc1
                 for u in ROUNDS[i + 1]:
                     prepare(u)
             for r in ROUNDS[i]:
-                for t in range(PACK) if r in (0, UNITS - 1) else READ_ORDER if r == ROUNDS[i][0] else LATER_ORDER:
-                    read_bank(r * PACK + t)
-                    was_read.add(r * PACK + t)
+                for b in range(r * PACK // PAIR, (r + 1) * PACK // PAIR):
+                    read_bank(b)
+                    was_read.add(b)
                     refill()
                 if r == NORM2_AT:
                     norm_root(0)

@@ -31,7 +31,8 @@ S_COLS_EARLY = 288
 WARM_FIRST = 8
 WARM_SECOND = 5
 WARM_LAST = 8
-S_COLS = 352
+S_COLS = 368
+RUN = 4
 BN_EPS = 1e-5
 NORM2_AT = 16
 
@@ -189,7 +190,11 @@ def tile_p2b_xcorr_pb_kernel(tc, h2, W3, g3, b3, m3, v3, Wc1, gc1, bc1, mc1, vc1
 
         def interleave_most(u):
             grouped = grpp.tile([P, UNIT, PACK], BF16, tag="grouped", align_bytes=64)
-            nc.scalar.copy(out=grouped[:, 0 : s_end(u), :], in_=rows_of(u)[:, 0 : s_end(u), :])
+            raw, a = raw_of[u]
+            nc.scalar.copy(
+                out=grouped[:, 0 : s_end(u), :].rearrange("p (c i) j -> p c j i", i=RUN),
+                in_=raw[:, :, a : a + s_end(u)].rearrange("p j (c i) -> p c j i", i=RUN),
+            )
             grouped_of[u] = grouped
 
         def interleave_rest(u):

@@ -27,7 +27,7 @@ SINGLE = 4
 ROUNDS = tuple((u,) for u in range(SINGLE)) + tuple((u, u + 1) for u in range(SINGLE, UNITS, 2))
 GROUPED_BUFS = 4
 EARLY = 4
-S_COLS_EARLY = 288
+S_COLS_EARLY = 368
 WARM_FIRST = 8
 WARM_SECOND = 5
 WARM_LAST = 8
@@ -262,25 +262,27 @@ def tile_p2b_xcorr_pb_kernel(tc, h2, W3, g3, b3, m3, v3, Wc1, gc1, bc1, mc1, vc1
                 issued.append(len(issued))
 
 
-        def prepare(u):
-            quantize(u)
-            if u + GROUPED_BUFS < UNITS:
-                interleave(u + GROUPED_BUFS)
-            if u + GROUPED_BUFS == UNITS - 1:
+        def prepare(units):
+            for u in units:
+                quantize(u)
+                if u + GROUPED_BUFS < UNITS:
+                    interleave_most(u + GROUPED_BUFS)
+                refill()
+            for u in reversed(units):
+                if u + GROUPED_BUFS < UNITS:
+                    interleave_rest(u + GROUPED_BUFS)
+            if units[-1] + GROUPED_BUFS == UNITS - 1:
                 norm_gain_shift(0)
                 nc.gpsimd.tensor_tensor(out=gain_abs[:], in0=gain[0][:], in1=sign[:], op=ALU.mult)
                 norm_gain_shift(1)
-            refill()
 
         for u in range(GROUPED_BUFS):
             interleave(u)
-        for u in ROUNDS[0]:
-            prepare(u)
+        prepare(ROUNDS[0])
 
         for i in range(len(ROUNDS)):
             if i + 1 < len(ROUNDS):
-                for u in ROUNDS[i + 1]:
-                    prepare(u)
+                prepare(ROUNDS[i + 1])
             for r in ROUNDS[i]:
                 for b in range(r * PACK // PAIR, (r + 1) * PACK // PAIR):
                     read_bank(b)

@@ -23,15 +23,15 @@ LOADS = (UNIT,) * SHORT_LOADS + (2 * UNIT,) * ((UNITS - SHORT_LOADS) // 2)
 WC1_LOAD_AT = 12 * UNIT
 PAIR = 2
 AHEAD = 6
-SINGLE = 4
+SINGLE = UNITS
 ROUNDS = tuple((u,) for u in range(SINGLE)) + tuple((u, u + 1) for u in range(SINGLE, UNITS, 2))
-GROUPED_BUFS = 4
+GROUPED_BUFS = 2
 EARLY = 4
-S_COLS_EARLY = 368
+S_COLS_EARLY = 384
 WARM_FIRST = 8
 WARM_SECOND = 5
 WARM_LAST = 8
-S_COLS = 368
+S_COLS = 384
 RUN = 4
 BN_EPS = 1e-5
 NORM2_AT = 16

@@ -103,35 +103,32 @@ def tile_p2b_xcorr_pb_kernel(tc, h2, W3, g3, b3, m3, v3, Wc1, gc1, bc1, mc1, vc1
         nc.vector.tensor_scalar(out=sign[:], in0=prm[:, 0, 0:PACK], scalar1=0.0, scalar2=2.0, op0=ALU.is_ge, op1=ALU.mult)
         nc.vector.tensor_scalar(out=sign[:], in0=sign[:], scalar1=-1.0, scalar2=None, op0=ALU.add)
 
-        var_eps, std, rough, newton, rstd, gain, shift = {}, {}, {}, {}, {}, {}, {}
-        for k in range(2):
-            var_eps[k] = keep.tile([P, PACK], F32, name="var_eps%d" % k)
-            std[k] = keep.tile([P, PACK], F32, name="std%d" % k)
-            rough[k] = keep.tile([P, PACK], F32, name="rough%d" % k)
-            newton[k] = keep.tile([P, PACK], F32, name="newton%d" % k)
-            rstd[k] = keep.tile([P, PACK], F32, name="rstd%d" % k)
-            gain[k] = keep.tile([P, PACK], F32, name="gain%d" % k)
-            shift[k] = keep.tile([P, PACK], F32, name="shift%d" % k)
+        var_eps = keep.tile([P, 2, PACK], F32)
+        std = keep.tile([P, 2, PACK], F32)
+        rough = keep.tile([P, 2, PACK], F32)
+        newton = keep.tile([P, 2, PACK], F32)
+        rstd = keep.tile([P, 2, PACK], F32)
+        gain = keep.tile([P, 2, PACK], F32)
+        shift = keep.tile([P, 2, PACK], F32)
         gain_abs = keep.tile([P, PACK], F32)
 
-        def norm_root(k):
-            nc.gpsimd.tensor_scalar(
-                out=var_eps[k][:], in0=prm[:, 6 + k, 0:PACK], scalar1=1.0, scalar2=BN_EPS, op0=ALU.mult, op1=ALU.add
-            )
-            nc.scalar.activation(out=std[k][:], in_=var_eps[k][:], func=ACT.Sqrt)
+        def norm_root():
+            nc.gpsimd.tensor_scalar(out=var_eps[:], in0=prm[:, 6:8, 0:PACK], scalar1=1.0, scalar2=BN_EPS, op0=ALU.mult, op1=ALU.add)
+            nc.scalar.activation(out=std[:], in_=var_eps[:], func=ACT.Sqrt)
 
-        def norm_reciprocal(k):
-            nc.vector.reciprocal(out=rough[k][:], in_=std[k][:])
+        def norm_reciprocal():
+            nc.vector.reciprocal(out=rough[:], in_=std[:])
 
-        def norm_gain_shift(k):
+        def norm_gain_shift():
             tt = nc.gpsimd.tensor_tensor
-            tt(out=newton[k][:], in0=rough[k][:], in1=rough[k][:], op=ALU.mult)
-            tt(out=newton[k][:], in0=newton[k][:], in1=var_eps[k][:], op=ALU.mult)
-            nc.gpsimd.tensor_scalar(out=newton[k][:], in0=newton[k][:], scalar1=-0.5, scalar2=1.5, op0=ALU.mult, op1=ALU.add)
-            tt(out=rstd[k][:], in0=rough[k][:], in1=newton[k][:], op=ALU.mult)
-            tt(out=gain[k][:], in0=prm[:, k, 0:PACK], in1=rstd[k][:], op=ALU.mult)
-            tt(out=shift[k][:], in0=prm[:, 4 + k, 0:PACK], in1=gain[k][:], op=ALU.mult)
-            tt(out=shift[k][:], in0=prm[:, 2 + k, 0:PACK], in1=shift[k][:], op=ALU.subtract)
+            tt(out=newton[:], in0=rough[:], in1=rough[:], op=ALU.mult)
+            tt(out=newton[:], in0=newton[:], in1=var_eps[:], op=ALU.mult)
+            nc.gpsimd.tensor_scalar(out=newton[:], in0=newton[:], scalar1=-0.5, scalar2=1.5, op0=ALU.mult, op1=ALU.add)
+            tt(out=rstd[:], in0=rough[:], in1=newton[:], op=ALU.mult)
+            tt(out=gain[:], in0=prm[:, 0:2, 0:PACK], in1=rstd[:], op=ALU.mult)
+            tt(out=gain_abs[:], in0=gain[:, 0, :], in1=sign[:], op=ALU.mult)
+            tt(out=shift[:], in0=prm[:, 4:6, 0:PACK], in1=gain[:], op=ALU.mult)
+            tt(out=shift[:], in0=prm[:, 2:4, 0:PACK], in1=shift[:], op=ALU.subtract)
 
         w3_signed = keep.tile([P, PACK, H], BF16)
         for t in range(PACK):
@@ -219,14 +216,17 @@ def tile_p2b_xcorr_pb_kernel(tc, h2, W3, g3, b3, m3, v3, Wc1, gc1, bc1, mc1, vc1
             )
             codes_of[u] = (codes, scales)
 
+        def first_block(b):
+            return PAIR * ((b + b // 2) % 2)
+
         def multiply(s):
-            u, t = divmod(s, PACK)
-            codes, scales = codes_of[u]
-            if t % PAIR == 0:
+            codes, scales = codes_of[s // PACK]
+            t = first_block(s // PAIR) + s % PAIR
+            if s % PAIR == 0:
                 bank = psum.tile([P, PAIR, UNIT], BF16, tag="x3")
                 bank_of[s // PAIR] = bank
             nc.tensor.matmul_mx(
-                out=bank_of[s // PAIR][:, t % PAIR, :],
+                out=bank_of[s // PAIR][:, s % PAIR, :],
                 lhsT=w3_codes[:, t * P : (t + 1) * P].bitcast(FP8X4),
                 lhsT_scale=w3_scales[:, t * P : (t + 1) * P],
                 rhs=codes[:].bitcast(FP8X4),
@@ -241,13 +241,18 @@ def tile_p2b_xcorr_pb_kernel(tc, h2, W3, g3, b3, m3, v3, Wc1, gc1, bc1, mc1, vc1
         top = tops[UNITS % 2]
 
         def read_bank(b):
-            u, t = divmod(b * PAIR, PACK)
+            u, t = b // 2, first_block(b)
             if u == 0:
                 nc.vector.tensor_copy(out=tops[1][:, t : t + PAIR, :], in_=bank_of[b][:])
             else:
                 nc.vector.tensor_tensor(
                     out=tops[(u + 1) % 2][:, t : t + PAIR, :], in0=bank_of[b][:], in1=tops[u % 2][:, t : t + PAIR, :], op=ALU.max
                 )
+
+        def reads_of(u):
+            if u in (0, UNITS - 1):
+                return (2 * u, 2 * u + 1)
+            return (2 * u + 1, 2 * u)
 
         was_read = set()
         issued = []
@@ -272,9 +277,7 @@ def tile_p2b_xcorr_pb_kernel(tc, h2, W3, g3, b3, m3, v3, Wc1, gc1, bc1, mc1, vc1
                 if u + GROUPED_BUFS < UNITS:
                     interleave_rest(u + GROUPED_BUFS)
             if units[-1] + GROUPED_BUFS == UNITS - 1:
-                norm_gain_shift(0)
-                nc.gpsimd.tensor_tensor(out=gain_abs[:], in0=gain[0][:], in1=sign[:], op=ALU.mult)
-                norm_gain_shift(1)
+                norm_gain_shift()
 
         for u in range(GROUPED_BUFS):
             interleave(u)
@@ -284,37 +287,36 @@ def tile_p2b_xcorr_pb_kernel(tc, h2, W3, g3, b3, m3, v3, Wc1, gc1, bc1, mc1, vc1
             if i + 1 < len(ROUNDS):
                 prepare(ROUNDS[i + 1])
             for r in ROUNDS[i]:
-                for b in range(r * PACK // PAIR, (r + 1) * PACK // PAIR):
+                for b in reads_of(r):
                     read_bank(b)
                     was_read.add(b)
                     refill()
                 if r == NORM2_AT:
-                    norm_root(0)
-                    norm_root(1)
+                    norm_root()
                 if r == NORM2_AT + 2:
-                    norm_reciprocal(0)
-                    norm_reciprocal(1)
+                    norm_reciprocal()
                 if r == UNITS - 2:
                     wc1_grouped = group_weights(turn_weights(wc1_rows), nc.scalar.copy)
                     keep_warm(WARM_LAST)
 
+        fold_order = tuple(first_block(b) for b in reads_of(UNITS - 1))
         half = keep.tile([P, PACK, 2 * NPTS], BF16)
         peak = keep.tile([P, PACK, NPTS], BF16)
         linear = keep.tile([P, PACK, NPTS], F32)
-        for t in (0, 2):
+        for t in fold_order:
             nc.vector.tensor_tensor(
                 out=half[:, t : t + 2, :], in0=top[:, t : t + 2, 0 : 2 * NPTS], in1=top[:, t : t + 2, 2 * NPTS : UNIT], op=ALU.max
             )
-        for t in (0, 2):
+        for t in fold_order:
             nc.vector.tensor_tensor(
                 out=peak[:, t : t + 2, :], in0=half[:, t : t + 2, 0:NPTS], in1=half[:, t : t + 2, NPTS : 2 * NPTS], op=ALU.max
             )
-        for t in range(PACK):
+        for t in tuple(first + i for first in fold_order for i in range(PAIR)):
             nc.vector.tensor_scalar(
                 out=linear[:, t, :],
                 in0=peak[:, t, :],
                 scalar1=gain_abs[:, t : t + 1],
-                scalar2=shift[0][:, t : t + 1],
+                scalar2=shift[:, 0, t : t + 1],
                 op0=ALU.mult,
                 op1=ALU.add,
             )
@@ -353,6 +355,6 @@ def tile_p2b_xcorr_pb_kernel(tc, h2, W3, g3, b3, m3, v3, Wc1, gc1, bc1, mc1, vc1
             for i in range(2):
                 t = 2 * b + i
                 nc.scalar.activation(
-                    out=result[:, i, :], in_=xc[t][:], func=ACT.Relu, bias=shift[1][:, t : t + 1], scale=gain[1][:, t : t + 1]
+                    out=result[:, i, :], in_=xc[t][:], func=ACT.Relu, bias=shift[:, 1, t : t + 1], scale=gain[:, 1, t : t + 1]
                 )
             (nc.sync if b == 0 else nc.scalar).dma_start(out=out_rows[:, 2 * b : 2 * b + 2, :], in_=result[:])

@@ -29,7 +29,7 @@ GROUPED_BUFS = 2
 EARLY = 4
 S_COLS_EARLY = 384
 WARM_FIRST = 8
-WARM_SECOND = 5
+WARM_SECOND = 2
 WARM_LAST = 8
 S_COLS = 384
 RUN = 4
@@ -72,7 +72,6 @@ def tile_p2b_xcorr_pb_kernel(tc, h2, W3, g3, b3, m3, v3, Wc1, gc1, bc1, mc1, vc1
         w3_rows = {}
         for b in range(2):
             w3_rows[b] = keep.tile([P, 2, H], BF16, name="w3_rows%d" % b)
-            nc.sync.dma_start(out=w3_rows[b][:], in_=W3.rearrange("(m t) h -> m t h", t=PACK)[:, 2 * b : 2 * b + 2, :])
         wc1_rows = keep.tile([P, PACK, H], BF16)
 
         h2_rows = h2[0].rearrange("(p j) m n -> p j (m n)", j=PACK)
@@ -84,6 +83,9 @@ def tile_p2b_xcorr_pb_kernel(tc, h2, W3, g3, b3, m3, v3, Wc1, gc1, bc1, mc1, vc1
             for a in range(0, width, UNIT):
                 raw_of[(first + a) // UNIT] = (raw, a)
             first += width
+            if first == UNIT:
+                for b in range(2):
+                    nc.sync.dma_start(out=w3_rows[b][:], in_=W3.rearrange("(m t) h -> m t h", t=PACK)[:, 2 * b : 2 * b + 2, :])
             if first == WC1_LOAD_AT:
                 nc.sync.dma_start(out=wc1_rows[:], in_=Wc1.rearrange("(m t) h -> m t h", t=PACK))
                 load_vector(nc.sync, 6, v3)
@@ -171,8 +173,7 @@ def tile_p2b_xcorr_pb_kernel(tc, h2, W3, g3, b3, m3, v3, Wc1, gc1, bc1, mc1, vc1
                 in_=grouped_w[:, b * PACK * H // 2 : (b + 1) * PACK * H // 2],
             )
 
-        group_weights(turn_weights(w3_signed), nc.vector.tensor_copy, quantize_w3_half)
-        keep_warm(WARM_SECOND)
+        w3_turned = turn_weights(w3_signed)
 
         grouped_of = {}
         codes_of = {}
@@ -281,7 +282,11 @@ def tile_p2b_xcorr_pb_kernel(tc, h2, W3, g3, b3, m3, v3, Wc1, gc1, bc1, mc1, vc1
 
         for u in range(GROUPED_BUFS):
             interleave(u)
-        prepare(ROUNDS[0])
+        quantize(0)
+        interleave(GROUPED_BUFS)
+        group_weights(w3_turned, nc.vector.tensor_copy, quantize_w3_half)
+        keep_warm(WARM_SECOND)
+        refill()
 
         for i in range(len(ROUNDS)):
             if i + 1 < len(ROUNDS):

@@ -35,6 +35,7 @@ S_COLS = 384
 RUN = 4
 BN_EPS = 1e-5
 NORM2_AT = 16
+V_HELP = {0: 256}
 
 FLOPS = 2 * H * H * (COLS + NPTS)
 
@@ -133,10 +134,12 @@ def tile_p2b_xcorr_pb_kernel(tc, h2, W3, g3, b3, m3, v3, Wc1, gc1, bc1, mc1, vc1
             tt(out=shift[:], in0=prm[:, 2:4, 0:PACK], in1=shift[:], op=ALU.subtract)
 
         w3_signed = keep.tile([P, PACK, H], BF16)
-        for t in range(PACK):
-            nc.vector.tensor_scalar(
-                out=w3_signed[:, t, :], in0=w3_rows[t // 2][:, t % 2, :], scalar1=sign[:, t : t + 1], scalar2=None, op0=ALU.mult
-            )
+
+        def sign_weights():
+            for t in range(PACK):
+                nc.vector.tensor_scalar(
+                    out=w3_signed[:, t, :], in0=w3_rows[t // 2][:, t % 2, :], scalar1=sign[:, t : t + 1], scalar2=None, op0=ALU.mult
+                )
 
         def turn_weights(rows):
             halves = []
@@ -173,8 +176,6 @@ def tile_p2b_xcorr_pb_kernel(tc, h2, W3, g3, b3, m3, v3, Wc1, gc1, bc1, mc1, vc1
                 in_=grouped_w[:, b * PACK * H // 2 : (b + 1) * PACK * H // 2],
             )
 
-        w3_turned = turn_weights(w3_signed)
-
         grouped_of = {}
         codes_of = {}
         bank_of = {}
@@ -184,7 +185,7 @@ def tile_p2b_xcorr_pb_kernel(tc, h2, W3, g3, b3, m3, v3, Wc1, gc1, bc1, mc1, vc1
             return raw[:, :, a : a + UNIT].rearrange("p j c -> p c j")
 
         def s_end(u):
-            return S_COLS_EARLY if u < EARLY else S_COLS
+            return UNIT - V_HELP[u] if u in V_HELP else S_COLS
 
         def interleave_most(u):
             grouped = grpp.tile([P, UNIT, PACK], BF16, tag="grouped", align_bytes=64)
@@ -196,6 +197,13 @@ def tile_p2b_xcorr_pb_kernel(tc, h2, W3, g3, b3, m3, v3, Wc1, gc1, bc1, mc1, vc1
             grouped_of[u] = grouped
 
         def interleave_rest(u):
+            if u in V_HELP:
+                raw, a = raw_of[u]
+                nc.vector.tensor_copy(
+                    out=grouped_of[u][:, s_end(u) : UNIT, :].rearrange("p (c i) j -> p c j i", i=RUN),
+                    in_=raw[:, :, a + s_end(u) : a + UNIT].rearrange("p j (c i) -> p c j i", i=RUN),
+                )
+                return
             nc.gpsimd.tensor_scalar(
                 out=grouped_of[u][:, s_end(u) : UNIT, :],
                 in0=rows_of(u)[:, s_end(u) : UNIT, :],
@@ -280,8 +288,10 @@ def tile_p2b_xcorr_pb_kernel(tc, h2, W3, g3, b3, m3, v3, Wc1, gc1, bc1, mc1, vc1
             if units[-1] + GROUPED_BUFS == UNITS - 1:
                 norm_gain_shift()
 
-        for u in range(GROUPED_BUFS):
-            interleave(u)
+        interleave(0)
+        sign_weights()
+        w3_turned = turn_weights(w3_signed)
+        interleave(1)
         quantize(0)
         interleave(GROUPED_BUFS)
         group_weights(w3_turned, nc.vector.tensor_copy, quantize_w3_half)

from contextlib import ExitStack

import concourse.mybir as mybir
from concourse.masks import make_identity

F32 = mybir.dt.float32
BF16 = mybir.dt.bfloat16
U32 = mybir.dt.uint32
U8 = mybir.dt.uint8
FP8X4 = mybir.dt.float8_e4m3fn_x4
ALU = mybir.AluOpType
ACT = mybir.ActivationFunctionType

P = 128
PACK = 4
H = 512
NPTS = 128
COLS = NPTS * NPTS
UNIT = 512
UNITS = COLS // UNIT
SHORT_LOADS = 6
LOADS = (UNIT,) * SHORT_LOADS + (2 * UNIT,) * ((UNITS - SHORT_LOADS) // 2)
WC1_LOAD_AT = 12 * UNIT
PAIR = 2
AHEAD = 6
SINGLE = UNITS
ROUNDS = tuple((u,) for u in range(SINGLE)) + tuple((u, u + 1) for u in range(SINGLE, UNITS, 2))
GROUPED_BUFS = 2
EARLY = 4
S_COLS_EARLY = 384
WARM_FIRST = 8
WARM_SECOND = 2
WARM_LAST = 8
S_COLS = 384
RUN = 4
BN_EPS = 1e-5
NORM2_AT = 16
V_HELP = {0: 256}

FLOPS = 2 * H * H * (COLS + NPTS)


def tile_p2b_xcorr_pb_kernel(tc, h2, W3, g3, b3, m3, v3, Wc1, gc1, bc1, mc1, vc1, out):
    nc = tc.nc
    with ExitStack() as ctx:
        keep = ctx.enter_context(tc.tile_pool(name="keep", bufs=1))
        rawp = ctx.enter_context(tc.tile_pool(name="rawp", bufs=1))
        grpp = ctx.enter_context(tc.tile_pool(name="grpp", bufs=GROUPED_BUFS))
        codp = ctx.enter_context(tc.tile_pool(name="codp", bufs=3))
        psum = ctx.enter_context(tc.psum_pool(name="psum", bufs=AHEAD))
        ctx.enter_context(tc.manual_schedule())

        prm = keep.tile([P, 8, 16], BF16)

        def load_vector(queue, slot, vec):
            queue.dma_start(out=prm[:, slot, 0:PACK], in_=vec.rearrange("(p t) -> p t", t=PACK))

        load_vector(nc.scalar, 0, g3)

        ident = keep.tile([P, P], F32)
        make_identity(nc, ident[:])

        zeros = keep.tile([P, UNIT], BF16)
        nc.vector.memset(zeros[:], 0.0)

        def keep_warm(passes):
            idle = psum.tile([P, UNIT], F32, tag="aux", bufs=2)
            for i in range(passes):
                nc.tensor.matmul(out=idle[:], lhsT=zeros[:, 0:P], rhs=zeros[:], start=True, stop=True)

        keep_warm(WARM_FIRST)

        w3_rows = {}
        for b in range(2):
            w3_rows[b] = keep.tile([P, 2, H], BF16, name="w3_rows%d" % b)
        wc1_rows = keep.tile([P, PACK, H], BF16)

        h2_rows = h2[0].rearrange("(p j) m n -> p j (m n)", j=PACK)
        raw_of = {}
        first = 0
        for width in LOADS:
            raw = rawp.tile([P, PACK, width], BF16, tag="raw%d" % width, bufs=SHORT_LOADS if width == UNIT else len(LOADS) - SHORT_LOADS)
            nc.sync.dma_start(out=raw[:], in_=h2_rows[:, :, first : first + width])
            for a in range(0, width, UNIT):
                raw_of[(first + a) // UNIT] = (raw, a)
            first += width
            if first == UNIT:
                for b in range(2):
                    nc.sync.dma_start(out=w3_rows[b][:], in_=W3.rearrange("(m t) h -> m t h", t=PACK)[:, 2 * b : 2 * b + 2, :])
            if first == WC1_LOAD_AT:
                nc.sync.dma_start(out=wc1_rows[:], in_=Wc1.rearrange("(m t) h -> m t h", t=PACK))
                load_vector(nc.sync, 6, v3)
                load_vector(nc.sync, 7, vc1)
                load_vector(nc.sync, 2, b3)
                load_vector(nc.sync, 4, m3)
                load_vector(nc.sync, 1, gc1)
                load_vector(nc.sync, 3, bc1)
                load_vector(nc.sync, 5, mc1)

        one = keep.tile([P, 1], F32)
        nc.vector.memset(one[:], 1.0)
        warm = keep.tile([P, 1], F32)
        nc.scalar.activation(out=warm[:], in_=one[:], func=ACT.Sqrt)

        sign = keep.tile([P, PACK], F32)
        nc.vector.tensor_scalar(out=sign[:], in0=prm[:, 0, 0:PACK], scalar1=0.0, scalar2=2.0, op0=ALU.is_ge, op1=ALU.mult)
        nc.vector.tensor_scalar(out=sign[:], in0=sign[:], scalar1=-1.0, scalar2=None, op0=ALU.add)

        var_eps = keep.tile([P, 2, PACK], F32)
        std = keep.tile([P, 2, PACK], F32)
        rough = keep.tile([P, 2, PACK], F32)
        newton = keep.tile([P, 2, PACK], F32)
        rstd = keep.tile([P, 2, PACK], F32)
        gain = keep.tile([P, 2, PACK], F32)
        shift = keep.tile([P, 2, PACK], F32)
        gain_abs = keep.tile([P, PACK], F32)

        def norm_root():
            nc.gpsimd.tensor_scalar(out=var_eps[:], in0=prm[:, 6:8, 0:PACK], scalar1=1.0, scalar2=BN_EPS, op0=ALU.mult, op1=ALU.add)
            nc.scalar.activation(out=std[:], in_=var_eps[:], func=ACT.Sqrt)

        def norm_reciprocal():
            nc.vector.reciprocal(out=rough[:], in_=std[:])

        def norm_gain_shift():
            tt = nc.gpsimd.tensor_tensor
            tt(out=newton[:], in0=rough[:], in1=rough[:], op=ALU.mult)
            tt(out=newton[:], in0=newton[:], in1=var_eps[:], op=ALU.mult)
            nc.gpsimd.tensor_scalar(out=newton[:], in0=newton[:], scalar1=-0.5, scalar2=1.5, op0=ALU.mult, op1=ALU.add)
            tt(out=rstd[:], in0=rough[:], in1=newton[:], op=ALU.mult)
            tt(out=gain[:], in0=prm[:, 0:2, 0:PACK], in1=rstd[:], op=ALU.mult)
            tt(out=gain_abs[:], in0=gain[:, 0, :], in1=sign[:], op=ALU.mult)
            tt(out=shift[:], in0=prm[:, 4:6, 0:PACK], in1=gain[:], op=ALU.mult)
            tt(out=shift[:], in0=prm[:, 2:4, 0:PACK], in1=shift[:], op=ALU.subtract)

        w3_signed = keep.tile([P, PACK, H], BF16)

        def sign_weights():
            for t in range(PACK):
                nc.vector.tensor_scalar(
                    out=w3_signed[:, t, :], in0=w3_rows[t // 2][:, t % 2, :], scalar1=sign[:, t : t + 1], scalar2=None, op0=ALU.mult
                )

        def turn_weights(rows):
            halves = []
            for b in range(2):
                turned = psum.tile([P, 2, 2, P], F32, tag="aux", bufs=2)
                for i in range(2):
                    words = rows[:, 2 * b + i, :].bitcast(F32)
                    for u in range(2):
                        nc.tensor.transpose(turned[:, i, u, :], words[:, u : H // 2 : 2], ident[:])
                halves.append(turned)
            return halves

        def group_weights(halves, copy, then=None):
            grouped_w = keep.tile([P, PACK * H], BF16, align_bytes=64)
            words_out = grouped_w[:].bitcast(F32).rearrange("p (t m u) -> p t m u", t=PACK, u=2)
            for b in range(2):
                copy(out=words_out[:, 2 * b : 2 * b + 2, :, :], in_=halves[b][:].rearrange("p t u m -> p t m u"))
                if then is not None:
                    then(grouped_w, b)
            return grouped_w

        def quantize_weights(grouped_w, codes, scales):
            nc.vector.quantize_mx(out=codes[:].bitcast(FP8X4), scales=scales[:], in_=grouped_w[:])

        w3_codes = keep.tile([P, H], U32, align_bytes=64)
        w3_scales = keep.tile([P, H], U8, align_bytes=64)
        wc1_codes = keep.tile([P, H], U32, align_bytes=64)
        wc1_scales = keep.tile([P, H], U8, align_bytes=64)

        def quantize_w3_half(grouped_w, b):
            nc.vector.quantize_mx(
                out=w3_codes[:, b * H // 2 : (b + 1) * H // 2].bitcast(FP8X4),
                scales=w3_scales[:, b * H // 2 : (b + 1) * H // 2],
                in_=grouped_w[:, b * PACK * H // 2 : (b + 1) * PACK * H // 2],
            )

        grouped_of = {}
        codes_of = {}
        bank_of = {}

        def rows_of(u):
            raw, a = raw_of[u]
            return raw[:, :, a : a + UNIT].rearrange("p j c -> p c j")

        def s_end(u):
            return UNIT - V_HELP[u] if u in V_HELP else S_COLS

        def interleave_most(u):
            grouped = grpp.tile([P, UNIT, PACK], BF16, tag="grouped", align_bytes=64)
            raw, a = raw_of[u]
            nc.scalar.copy(
                out=grouped[:, 0 : s_end(u), :].rearrange("p (c i) j -> p c j i", i=RUN),
                in_=raw[:, :, a : a + s_end(u)].rearrange("p j (c i) -> p c j i", i=RUN),
            )
            grouped_of[u] = grouped

        def interleave_rest(u):
            if u in V_HELP:
                raw, a = raw_of[u]
                nc.vector.tensor_copy(
                    out=grouped_of[u][:, s_end(u) : UNIT, :].rearrange("p (c i) j -> p c j i", i=RUN),
                    in_=raw[:, :, a + s_end(u) : a + UNIT].rearrange("p j (c i) -> p c j i", i=RUN),
                )
                return
            nc.gpsimd.tensor_scalar(
                out=grouped_of[u][:, s_end(u) : UNIT, :],
                in0=rows_of(u)[:, s_end(u) : UNIT, :],
                scalar1=1.0,
                scalar2=0.0,
                op0=ALU.mult,
                op1=ALU.add,
            )

        def interleave(u):
            interleave_most(u)
            interleave_rest(u)

        def quantize(u):
            codes = codp.tile([P, UNIT], U32, tag="codes", align_bytes=64)
            scales = codp.tile([P, UNIT], U8, tag="scales", align_bytes=64)
            nc.vector.quantize_mx(
                out=codes[:].bitcast(FP8X4), scales=scales[:], in_=grouped_of[u][:].rearrange("p c j -> p (c j)")
            )
            codes_of[u] = (codes, scales)

        def first_block(b):
            return PAIR * ((b + b // 2) % 2)

        def multiply(s):
            codes, scales = codes_of[s // PACK]
            t = first_block(s // PAIR) + s % PAIR
            if s % PAIR == 0:
                bank = psum.tile([P, PAIR, UNIT], BF16, tag="x3")
                bank_of[s // PAIR] = bank
            nc.tensor.matmul_mx(
                out=bank_of[s // PAIR][:, s % PAIR, :],
                lhsT=w3_codes[:, t * P : (t + 1) * P].bitcast(FP8X4),
                lhsT_scale=w3_scales[:, t * P : (t + 1) * P],
                rhs=codes[:].bitcast(FP8X4),
                rhs_scale=scales[:],
                start=True,
                stop=True,
            )

        tops = {}
        for k in range(2):
            tops[k] = keep.tile([P, PACK, UNIT], BF16, name="top%d" % k)
        top = tops[UNITS % 2]

        def read_bank(b):
            u, t = b // 2, first_block(b)
            if u == 0:
                nc.vector.tensor_copy(out=tops[1][:, t : t + PAIR, :], in_=bank_of[b][:])
            else:
                nc.vector.tensor_tensor(
                    out=tops[(u + 1) % 2][:, t : t + PAIR, :], in0=bank_of[b][:], in1=tops[u % 2][:, t : t + PAIR, :], op=ALU.max
                )

        def reads_of(u):
            if u in (0, UNITS - 1):
                return (2 * u, 2 * u + 1)
            return (2 * u + 1, 2 * u)

        was_read = set()
        issued = []

        def refill():
            while (
                len(issued) < UNITS * PACK
                and len(issued) // PACK in codes_of
                and (len(issued) // PAIR < AHEAD or len(issued) // PAIR - AHEAD in was_read)
            ):
                multiply(len(issued))
                issued.append(len(issued))


        def prepare(units):
            for u in units:
                quantize(u)
                if u + GROUPED_BUFS < UNITS:
                    interleave_most(u + GROUPED_BUFS)
                refill()
            for u in reversed(units):
                if u + GROUPED_BUFS < UNITS:
                    interleave_rest(u + GROUPED_BUFS)
            if units[-1] + GROUPED_BUFS == UNITS - 1:
                norm_gain_shift()

        interleave(0)
        sign_weights()
        w3_turned = turn_weights(w3_signed)
        interleave(1)
        quantize(0)
        interleave(GROUPED_BUFS)
        group_weights(w3_turned, nc.vector.tensor_copy, quantize_w3_half)
        keep_warm(WARM_SECOND)
        refill()

        for i in range(len(ROUNDS)):
            if i + 1 < len(ROUNDS):
                prepare(ROUNDS[i + 1])
            for r in ROUNDS[i]:
                for b in reads_of(r):
                    read_bank(b)
                    was_read.add(b)
                    refill()
                if r == NORM2_AT:
                    norm_root()
                if r == NORM2_AT + 2:
                    norm_reciprocal()
                if r == UNITS - 2:
                    wc1_grouped = group_weights(turn_weights(wc1_rows), nc.scalar.copy)
                    keep_warm(WARM_LAST)

        fold_order = tuple(first_block(b) for b in reads_of(UNITS - 1))
        half = keep.tile([P, PACK, 2 * NPTS], BF16)
        peak = keep.tile([P, PACK, NPTS], BF16)
        linear = keep.tile([P, PACK, NPTS], F32)
        for t in fold_order:
            nc.vector.tensor_tensor(
                out=half[:, t : t + 2, :], in0=top[:, t : t + 2, 0 : 2 * NPTS], in1=top[:, t : t + 2, 2 * NPTS : UNIT], op=ALU.max
            )
        for t in fold_order:
            nc.vector.tensor_tensor(
                out=peak[:, t : t + 2, :], in0=half[:, t : t + 2, 0:NPTS], in1=half[:, t : t + 2, NPTS : 2 * NPTS], op=ALU.max
            )
        for t in tuple(first + i for first in fold_order for i in range(PAIR)):
            nc.vector.tensor_scalar(
                out=linear[:, t, :],
                in0=peak[:, t, :],
                scalar1=gain_abs[:, t : t + 1],
                scalar2=shift[:, 0, t : t + 1],
                op0=ALU.mult,
                op1=ALU.add,
            )

        def quantize_wc1_half(b):
            nc.vector.quantize_mx(
                out=wc1_codes[:, b * H // 2 : (b + 1) * H // 2].bitcast(FP8X4),
                scales=wc1_scales[:, b * H // 2 : (b + 1) * H // 2],
                in_=wc1_grouped[:, b * PACK * H // 2 : (b + 1) * PACK * H // 2],
            )

        quantize_wc1_half(0)
        p_grouped = keep.tile([P, NPTS, PACK], BF16, align_bytes=64)
        nc.vector.tensor_scalar(out=p_grouped[:], in0=linear[:].rearrange("p t n -> p n t"), scalar1=0.0, scalar2=None, op0=ALU.max)
        quantize_wc1_half(1)
        p_codes = keep.tile([P, NPTS], U32, align_bytes=64)
        p_scales = keep.tile([P, NPTS], U8, align_bytes=64)
        nc.vector.quantize_mx(
            out=p_codes[:].bitcast(FP8X4), scales=p_scales[:], in_=p_grouped[:].rearrange("p n t -> p (n t)")
        )
        xc = {}
        for t in range(PACK):
            xc[t] = psum.tile([P, NPTS], F32, tag="x3", name="xc%d" % t)
            nc.tensor.matmul_mx(
                out=xc[t][:],
                lhsT=wc1_codes[:, t * P : (t + 1) * P].bitcast(FP8X4),
                lhsT_scale=wc1_scales[:, t * P : (t + 1) * P],
                rhs=p_codes[:].bitcast(FP8X4),
                rhs_scale=p_scales[:],
                start=True,
                stop=True,
            )
        out_rows = out[0].rearrange("(m t) n -> m t n", t=PACK)
        for b in range(2):
            result = keep.tile([P, 2, NPTS], F32, name="result%d" % b)
            for i in range(2):
                t = 2 * b + i
                nc.scalar.activation(
                    out=result[:, i, :], in_=xc[t][:], func=ACT.Relu, bias=shift[:, 1, t : t + 1], scale=gain[:, 1, t : t + 1]
                )
            (nc.sync if b == 0 else nc.scalar).dma_start(out=out_rows[:, 2 * b : 2 * b + 2, :], in_=result[:])
